import numpy as np
import ml_dtypes


def mxq(x, axis, fmt="e4m3"):
    dtype, down = {"e4m3": (ml_dtypes.float8_e4m3fn, 7), "e5m2": (ml_dtypes.float8_e5m2, 14)}[fmt]
    v = np.moveaxis(np.asarray(x, np.float32).astype(ml_dtypes.bfloat16).astype(np.float64), axis, -1)
    blocks = v.reshape(v.shape[:-1] + (-1, 32))
    amax = np.abs(blocks).max(-1, keepdims=True)
    byte = np.maximum(np.where(amax > 0, np.frexp(amax)[1] - 1 + 127, 0) - down, 1)
    scale = np.exp2(byte - 127.0)
    codes = (blocks / scale).astype(np.float32).astype(dtype).astype(np.float64)
    return np.moveaxis((codes * scale).reshape(v.shape), -1, axis)


WIDE = False


def mx_kscale(k):
    if not WIDE:
        return np.ones(k)
    levels = np.array([10, -10, 5, -5, 0])
    if k % 512:
        return np.exp2(np.random.permutation(np.resize(levels, k // 32))).repeat(32)
    a = np.empty((k // 512, 16))
    for p in range(k // 512):
        a[p, :8] = np.random.permutation(np.resize(levels, 8))
        for g in range(8):
            far = levels[np.abs(levels - a[p, g]) >= 10]
            a[p, g + 8] = far[np.random.randint(len(far))]
    return np.exp2(a.ravel()).repeat(32)


BF16 = ml_dtypes.bfloat16


def bf(x):
    return np.asarray(x, np.float32).astype(BF16)


def f64(x):
    return np.asarray(x).astype(np.float64)


B, T, D, H, G, HD, W = 1, 512, 2560, 8, 4, 256, 256
EPS = 1e-6


def rmsnorm(u, w):
    var = np.mean(u * u, axis=-1, keepdims=True)
    return u * (1.0 / np.sqrt(var + EPS)) * (1.0 + w)


def draw0():
    s = mx_kscale(D)
    return {"x": bf(np.random.standard_normal((B, T, D)) * s),
            "Wq": bf(np.random.standard_normal((D, H * HD)) * 0.005 / np.sqrt(D) / s[:, None]),
            "Wk": bf(np.random.standard_normal((D, G * HD)) * 0.005 / np.sqrt(D) / s[:, None]),
            "Wv": bf(np.random.standard_normal((D, G * HD)) * 1.0 / np.sqrt(D) / s[:, None]),
            "q_scale": bf(np.random.standard_normal(HD) * 0.2),
            "k_scale": bf(np.random.standard_normal(HD) * 0.2)}


def core(x, Wq, Wk, Wv, q_scale, k_scale):
    xq = mxq(f64(x), 2, "e4m3")
    q = (xq @ mxq(f64(Wq), 0, "e4m3")).reshape(B, T, H, HD).transpose(0, 2, 1, 3)
    k = (xq @ mxq(f64(Wk), 0, "e4m3")).reshape(B, T, G, HD).transpose(0, 2, 1, 3)
    v = (xq @ mxq(f64(Wv), 0, "e4m3")).reshape(B, T, G, HD).transpose(0, 2, 1, 3)
    return rmsnorm(q, f64(q_scale)), rmsnorm(k, f64(k_scale)), v


def e4m3fn_bytes(y):
    return np.clip(np.asarray(y, np.float64), -448.0, 448.0).astype(np.float32).astype(ml_dtypes.float8_e4m3fn).view(np.uint8)


def e4m3fn_values(b):
    return np.asarray(b, np.uint8).view(ml_dtypes.float8_e4m3fn).astype(np.float64)


def setup_inputs():
    d = draw0()
    x0 = np.asarray(d['Wq']).astype(np.float64)
    s = (np.max(np.abs(x0), axis=(1,), keepdims=True) / 448.0).astype(np.float32)
    out = {}
    for k, v in d.items():
        if k == 'Wq':
            out['Wq_bytes'] = e4m3fn_bytes(x0 / s.astype(np.float64))
            out['Wq_scale'] = s
        else:
            out[k] = v
    return out


def reference(x, Wq_bytes, Wq_scale, Wk, Wv, q_scale, k_scale):
    return core(x, e4m3fn_values(Wq_bytes) * Wq_scale.astype(np.float64), Wk, Wv, q_scale, k_scale)

@@ -1,0 +1,296 @@
+from contextlib import ExitStack
+
+import concourse.mybir as mybir
+from concourse.masks import make_identity
+
+F32 = mybir.dt.float32
+BF16 = mybir.dt.bfloat16
+U32 = mybir.dt.uint32
+U8 = mybir.dt.uint8
+FP8 = mybir.dt.float8_e4m3fn
+FP8X4 = mybir.dt.float8_e4m3fn_x4
+ACT = mybir.ActivationFunctionType
+ALU = mybir.AluOpType
+
+P = 128
+PACK = 4
+K_PASS = P * PACK
+T = 512
+D = 2560
+PASSES = D // K_PASS
+M_TILES = T // P
+HD = 256
+CH = 512
+HEADS_CH = CH // HD
+NQ = 2048
+NKV = 1024
+EPS = 1e-6
+
+FLOPS = 2 * T * D * (NQ + 2 * NKV)
+
+V_COLS = {"q": 512, "k": 256, "v": 288}
+RUN = 4
+V_WIDEN = ((1, 3), (3, 3))
+X_STEP = 5
+
+
+def tile_groupedqueryattention_pa_kernel(
+    tc, x, Wq_bytes, Wq_scale, Wk, Wv, q_scale, k_scale, out_0, out_1, out_2
+):
+    nc = tc.nc
+    with ExitStack() as ctx:
+        const = ctx.enter_context(tc.tile_pool(name="const", bufs=1))
+        raw = ctx.enter_context(tc.tile_pool(name="raw", bufs=1))
+        work = ctx.enter_context(tc.tile_pool(name="work", bufs=2))
+        psum = ctx.enter_context(tc.psum_pool(name="psum", bufs=2))
+        ctx.enter_context(tc.manual_schedule(engines={mybir.EngineType.SP}))
+
+        qs_view = Wq_scale.rearrange("(g p t) o -> p g (t o)", p=P, t=PACK)
+        qs_first = const.tile([P, 1, PACK], F32, name="qs_first")
+        nc.scalar.dma_start(out=qs_first[:], in_=qs_view[:, 0:1, :])
+        qs_rest = const.tile([P, PASSES - 1, PACK], F32, name="qs_rest")
+        nc.scalar.dma_start(out=qs_rest[:], in_=qs_view[:, 1:PASSES, :])
+
+        def q_scale_column(g, t):
+            if g == 0:
+                return qs_first[:, 0, t : t + 1]
+            return qs_rest[:, g - 1, t : t + 1]
+
+        warm = const.tile([P, 1], F32, name="warm")
+        nc.vector.memset(warm[:], 1.0)
+        nc.scalar.activation(out=warm[:], in_=warm[:], func=ACT.Sqrt)
+
+        gain_rows = const.tile([P, 2 * HD], BF16, name="gain_rows")
+        nc.gpsimd.memset(gain_rows[:], 0.0)
+        nc.scalar.dma_start(out=gain_rows[0:1, 0:HD], in_=q_scale.rearrange("(o d) -> o d", o=1))
+        nc.scalar.dma_start(out=gain_rows[0:1, HD : 2 * HD], in_=k_scale.rearrange("(o d) -> o d", o=1))
+
+        wq_view = Wq_bytes.rearrange("(g p t) n -> g p t n", p=P, t=PACK)
+        wk_view = Wk.rearrange("(g p t) n -> g p t n", p=P, t=PACK)
+        wv_view = Wv.rearrange("(g p t) n -> g p t n", p=P, t=PACK)
+        x_view = x.rearrange("b (m p) k -> p (b m) k", p=P)
+
+        q_bytes = [raw.tile([P, PACK, NQ], U8, name="q_bytes%d" % g) for g in range(PASSES)]
+        x_raw = [raw.tile([P, M_TILES, K_PASS], BF16, name="x_raw%d" % g) for g in range(PASSES)]
+        k_raw = [raw.tile([P, PACK, NKV], BF16, name="k_raw%d" % g) for g in range(PASSES)]
+        v_raw = [raw.tile([P, PACK, NKV], BF16, name="v_raw%d" % g) for g in range(PASSES)]
+
+        half = NQ // 2
+        for t0 in (0, 2):
+            nc.sync.dma_start(out=q_bytes[0][:, t0 : t0 + 2, 0:half], in_=wq_view[0][:, t0 : t0 + 2, 0:half])
+        for g in range(1, PASSES):
+            nc.sync.dma_start(out=q_bytes[g][:, :, 0:half], in_=wq_view[g][:, :, 0:half])
+        for g in range(PASSES):
+            nc.sync.dma_start(out=x_raw[g][:], in_=x_view[:, :, g * K_PASS : (g + 1) * K_PASS])
+        for g in range(PASSES):
+            nc.sync.dma_start(out=q_bytes[g][:, :, half:NQ], in_=wq_view[g][:, :, half:NQ])
+
+        def late_loads(j):
+            if j == 0:
+                for g in range(PASSES):
+                    nc.sync.dma_start(out=k_raw[g][:], in_=wk_view[g])
+            if j == 1:
+                for g in range(PASSES):
+                    nc.sync.dma_start(out=v_raw[g][:], in_=wv_view[g])
+
+        ident = const.tile([P, P], F32, name="ident")
+        make_identity(nc, ident[:])
+        ones = const.tile([P, P], BF16, name="ones")
+        nc.gpsimd.memset(ones[:], 1.0)
+        gain_all = const.tile([P, 2 * HD], F32, name="gain_all")
+        gain = {"q": gain_all[:, 0:HD], "k": gain_all[:, HD : 2 * HD]}
+
+        def spread_gains():
+            gain_ps = psum.tile([P, 2 * HD], F32, name="gain_ps", tag="bank", bufs=8)
+            nc.tensor.matmul(out=gain_ps[:], lhsT=ones[:], rhs=gain_rows[:], start=True, stop=True)
+            nc.vector.tensor_scalar(
+                out=gain_all[:], in0=gain_ps[:], scalar1=1.0, scalar2=None, op0=ALU.add
+            )
+
+        x_codes = const.tile([P, PASSES, T], U32, name="x_codes", align_bytes=64)
+        x_scales = const.tile([P, PASSES, T], U8, name="x_scales", align_bytes=64)
+
+        x_grouped = {}
+
+        def x_turn(g):
+            xg = work.tile([P, T, PACK], BF16, name="xg", tag="xg", bufs=2, align_bytes=64)
+            x_grouped[g] = xg
+            xg_words = (
+                xg[:].rearrange("p r j -> p (r j)").bitcast(F32)
+                .rearrange("p (m r u) -> p m r u", m=M_TILES, u=2)
+            )
+            for pair in range(M_TILES // 2):
+                xt = psum.tile([P, 2, 2, P], F32, name="xt", tag="bank", bufs=8)
+                for mm in range(2):
+                    words = x_raw[g][:, 2 * pair + mm, :].bitcast(F32)
+                    for u in range(2):
+                        nc.tensor.transpose(xt[:, mm, u, :], words[:, u : K_PASS // 2 : 2], ident[:])
+                dst = xg_words[:, 2 * pair : 2 * pair + 2]
+                src = xt[:].rearrange("p m u r -> p m r u")
+                if pair == 0:
+                    nc.scalar.copy(out=dst, in_=src)
+                else:
+                    nc.vector.tensor_copy(out=dst, in_=src)
+
+        def x_quant(g):
+            nc.vector.quantize_mx(
+                out=x_codes[:, g, :].bitcast(FP8X4),
+                scales=x_scales[:, g, :],
+                in_=x_grouped[g][:].rearrange("p r j -> p (r j)"),
+            )
+
+        chunks = (
+            [("q", c) for c in range(NQ // CH)]
+            + [("k", c) for c in range(NKV // CH)]
+            + [("v", c) for c in range(NKV // CH)]
+        )
+        units = [(j, g) for j in range(len(chunks)) for g in range(PASSES)]
+        wide_t = {}
+        grouped_t = {}
+        codes_t = {}
+        acc_t = {}
+
+        def widen(j, g):
+            kind, c = chunks[j]
+            if kind != "q":
+                return
+            wide = work.tile([P, PACK, CH], BF16, name="wide", tag="wide", bufs=3)
+            wide_t[(j, g)] = wide
+            for t in range(PACK):
+                src = q_bytes[g][:, t, c * CH : (c + 1) * CH].bitcast(FP8)
+                on_vector = (g, t) in V_WIDEN or (j == 0 and g == 0 and t >= 2)
+                if on_vector:
+                    nc.vector.tensor_scalar(
+                        out=wide[:, t, :], in0=src, scalar1=q_scale_column(g, t), scalar2=None,
+                        op0=ALU.mult,
+                    )
+                else:
+                    nc.scalar.activation(
+                        out=wide[:, t, :], in_=src, func=ACT.Copy, scale=q_scale_column(g, t)
+                    )
+
+        def interleave(j, g):
+            kind, c = chunks[j]
+            if kind == "q":
+                src = wide_t[(j, g)][:]
+            elif kind == "k":
+                src = k_raw[g][:, :, c * CH : (c + 1) * CH]
+            else:
+                src = v_raw[g][:, :, c * CH : (c + 1) * CH]
+            wg = work.tile([P, CH, PACK], BF16, name="wg", tag="wg", bufs=4, align_bytes=64)
+            grouped_t[(j, g)] = wg
+            cv = V_COLS[kind]
+            nc.vector.tensor_copy(
+                out=wg[:, 0:cv, :].rearrange("p (c i) t -> p c t i", i=RUN),
+                in_=src[:, :, 0:cv].rearrange("p t (c i) -> p c t i", i=RUN),
+            )
+            if cv < CH:
+                nc.scalar.copy(
+                    out=wg[:, cv:CH, :].rearrange("p (c i) t -> p c t i", i=RUN),
+                    in_=src[:, :, cv:CH].rearrange("p t (c i) -> p c t i", i=RUN),
+                )
+
+        def quantize(j, g):
+            if g == 0:
+                wc = work.tile([P, PASSES, CH], U32, name="wc", tag="wc", bufs=2, align_bytes=64)
+                ws = work.tile([P, PASSES, CH], U8, name="ws", tag="ws", bufs=2, align_bytes=64)
+                codes_t[j] = (wc, ws)
+            wc, ws = codes_t[j]
+            nc.vector.quantize_mx(
+                out=wc[:, g, :].bitcast(FP8X4),
+                scales=ws[:, g, :],
+                in_=grouped_t[(j, g)][:].rearrange("p c t -> p (c t)"),
+            )
+
+        def matmuls(j, g):
+            if g == 0:
+                acc_t[j] = [
+                    psum.tile([P, CH], F32, name="acc", tag="bank", bufs=8) for m in range(M_TILES)
+                ]
+            wc, ws = codes_t[j]
+            for m in range(M_TILES):
+                cols = slice(m * P, (m + 1) * P)
+                nc.tensor.matmul_mx(
+                    out=acc_t[j][m][:],
+                    lhsT=x_codes[:, g, cols].bitcast(FP8X4),
+                    lhsT_scale=x_scales[:, g, cols],
+                    rhs=wc[:, g, :].bitcast(FP8X4),
+                    rhs_scale=ws[:, g, :],
+                    start=(g == 0),
+                    stop=(g == PASSES - 1),
+                )
+
+        out_views = {
+            "q": out_0.rearrange("b h (m p) d -> p (b h) m d", p=P),
+            "k": out_1.rearrange("b h (m p) d -> p (b h) m d", p=P),
+            "v": out_2.rearrange("b h (m p) d -> p (b h) m d", p=P),
+        }
+
+        def epilogue(j):
+            kind, c = chunks[j]
+            acc = acc_t[j]
+            heads = slice(c * HEADS_CH, (c + 1) * HEADS_CH)
+            if kind == "v":
+                for m in range(M_TILES):
+                    o = work.tile([P, HEADS_CH, HD], F32, name="o", tag="o", bufs=7)
+                    flat = o[:].rearrange("p h d -> p (h d)")
+                    if m % 2 == 0 or j < len(chunks) - 1:
+                        nc.scalar.copy(out=flat, in_=acc[m][:])
+                    else:
+                        nc.vector.tensor_copy(out=flat, in_=acc[m][:])
+                    nc.sync.dma_start(out=out_views[kind][:, heads, m, :], in_=o[:])
+                return
+            n = M_TILES * HEADS_CH
+            ssq = work.tile([P, n], F32, name="ssq", tag="ssq", bufs=2)
+            for m in range(M_TILES):
+                for h in range(HEADS_CH):
+                    junk = work.tile([P, HD], BF16, name="junk", tag="junk", bufs=2)
+                    i = m * HEADS_CH + h
+                    nc.scalar.activation(
+                        out=junk[:], in_=acc[m][:, h * HD : (h + 1) * HD], func=ACT.Square,
+                        accum_out=ssq[:, i : i + 1],
+                    )
+            rms = work.tile([P, n], F32, name="rms", tag="rms", bufs=2)
+            nc.scalar.activation(out=rms[:], in_=ssq[:], func=ACT.Sqrt, scale=1.0 / HD, bias=EPS)
+            rstd = work.tile([P, n], F32, name="rstd", tag="rstd", bufs=2)
+            nc.vector.reciprocal(out=rstd[:], in_=rms[:])
+            for m in range(M_TILES):
+                o = work.tile([P, HEADS_CH, HD], F32, name="o", tag="o", bufs=7)
+                for h in range(HEADS_CH):
+                    i = m * HEADS_CH + h
+                    nc.vector.scalar_tensor_tensor(
+                        out=o[:, h, :], in0=acc[m][:, h * HD : (h + 1) * HD],
+                        scalar=rstd[:, i : i + 1], in1=gain[kind],
+                        op0=ALU.mult, op1=ALU.mult,
+                    )
+                nc.sync.dma_start(out=out_views[kind][:, heads, m, :], in_=o[:])
+
+        n_units = len(units)
+        waiting = []
+        due = {}
+        x_done = False
+        for s in range(n_units + 5):
+            if s < n_units:
+                widen(*units[s])
+            if 1 <= s <= n_units:
+                interleave(*units[s - 1])
+            if 2 <= s <= n_units + 1:
+                quantize(*units[s - 2])
+                waiting.append(units[s - 2])
+            if s == X_STEP:
+                for g in range(PASSES):
+                    x_turn(g)
+                    if g >= 1:
+                        x_quant(g - 1)
+                x_quant(PASSES - 1)
+                spread_gains()
+                x_done = True
+            if x_done:
+                for u in waiting:
+                    matmuls(*u)
+                    if u[1] == PASSES - 1:
+                        due.setdefault(s + 1, []).append(u[0])
+                waiting = []
+            for j in due.get(s, []):
+                epilogue(j)
+                late_loads(j)

@@ -28,9 +28,11 @@ EPS = 1e-6
 
 FLOPS = 2 * T * D * (NQ + 2 * NKV)
 
-V_COLS = {"q": 512, "k": 256, "v": 288}
+V_COLS = {"q": 512, "k": 256, "v": 256}
 RUN = 4
 V_WIDEN = ((1, 3), (3, 3))
+G_COLS = 320
+G_V_COLS = 64
 X_STEP = 5
 
 
@@ -70,10 +72,10 @@ def tile_groupedqueryattention_pa_kernel(
         wv_view = Wv.rearrange("(g p t) n -> g p t n", p=P, t=PACK)
         x_view = x.rearrange("b (m p) k -> p (b m) k", p=P)
 
-        q_bytes = [raw.tile([P, PACK, NQ], U8, name="q_bytes%d" % g) for g in range(PASSES)]
+        q_bytes = [raw.tile([P, PACK, NQ], U8, name="q_bytes%d" % g, tag="qv%d" % g) for g in range(PASSES)]
         x_raw = [raw.tile([P, M_TILES, K_PASS], BF16, name="x_raw%d" % g) for g in range(PASSES)]
         k_raw = [raw.tile([P, PACK, NKV], BF16, name="k_raw%d" % g) for g in range(PASSES)]
-        v_raw = [raw.tile([P, PACK, NKV], BF16, name="v_raw%d" % g) for g in range(PASSES)]
+        v_raw = []
 
         half = NQ // 2
         for t0 in (0, 2):
@@ -82,15 +84,17 @@ def tile_groupedqueryattention_pa_kernel(
             nc.sync.dma_start(out=q_bytes[g][:, :, 0:half], in_=wq_view[g][:, :, 0:half])
         for g in range(PASSES):
             nc.sync.dma_start(out=x_raw[g][:], in_=x_view[:, :, g * K_PASS : (g + 1) * K_PASS])
+        nc.sync.dma_start(out=k_raw[0][:], in_=wk_view[0])
         for g in range(PASSES):
             nc.sync.dma_start(out=q_bytes[g][:, :, half:NQ], in_=wq_view[g][:, :, half:NQ])
 
         def late_loads(j):
             if j == 0:
-                for g in range(PASSES):
+                for g in range(1, PASSES):
                     nc.sync.dma_start(out=k_raw[g][:], in_=wk_view[g])
-            if j == 1:
+            if j == 2:
                 for g in range(PASSES):
+                    v_raw.append(raw.tile([P, PACK, NKV], BF16, name="v_raw%d" % g, tag="qv%d" % g))
                     nc.sync.dma_start(out=v_raw[g][:], in_=wv_view[g])
 
         ident = const.tile([P, P], F32, name="ident")
@@ -106,6 +110,11 @@ def tile_groupedqueryattention_pa_kernel(
             nc.vector.tensor_scalar(
                 out=gain_all[:], in0=gain_ps[:], scalar1=1.0, scalar2=None, op0=ALU.add
             )
+
+        n_sums = M_TILES * HEADS_CH
+        rms_tiles = [const.tile([P, n_sums + 1], F32, name="rms%d" % i) for i in range(2)]
+        for i in range(2):
+            nc.gpsimd.memset(rms_tiles[i][:], 1.0)
 
         x_codes = const.tile([P, PASSES, T], U32, name="x_codes", align_bytes=64)
         x_scales = const.tile([P, PASSES, T], U8, name="x_scales", align_bytes=64)
@@ -154,7 +163,7 @@ def tile_groupedqueryattention_pa_kernel(
             kind, c = chunks[j]
             if kind != "q":
                 return
-            wide = work.tile([P, PACK, CH], BF16, name="wide", tag="wide", bufs=3)
+            wide = work.tile([P, PACK, CH], BF16, name="wide", tag="wide", bufs=6)
             wide_t[(j, g)] = wide
             for t in range(PACK):
                 src = q_bytes[g][:, t, c * CH : (c + 1) * CH].bitcast(FP8)
@@ -169,20 +178,44 @@ def tile_groupedqueryattention_pa_kernel(
                         out=wide[:, t, :], in_=src, func=ACT.Copy, scale=q_scale_column(g, t)
                     )
 
-        def interleave(j, g):
+        def planes(j, g):
             kind, c = chunks[j]
             if kind == "q":
-                src = wide_t[(j, g)][:]
-            elif kind == "k":
-                src = k_raw[g][:, :, c * CH : (c + 1) * CH]
+                return wide_t[(j, g)][:]
+            if kind == "k":
+                return k_raw[g][:, :, c * CH : (c + 1) * CH]
+            return v_raw[g][:, :, c * CH : (c + 1) * CH]
+
+        def early_unit(j):
+            first_plain = NQ // CH
+            if j + 2 <= first_plain:
+                return (first_plain, j)
+            return (j + 2, 0)
+
+        def early_interleave(j, one):
+            u = early_unit(j)
+            wg = work.tile([P, CH, PACK], BF16, name="wg_early", tag="wg_early", bufs=4, align_bytes=64)
+            grouped_t[u] = wg
+            nc.gpsimd.tensor_scalar(
+                out=wg[:, 0:G_COLS, :], in0=planes(*u)[:, :, 0:G_COLS].rearrange("p t c -> p c t"),
+                scalar1=one, scalar2=0.0, op0=ALU.mult, op1=ALU.add,
+            )
+
+        def interleave(j, g):
+            kind, c = chunks[j]
+            src = planes(j, g)
+            if (j, g) in grouped_t:
+                wg = grouped_t[(j, g)]
+                c0 = G_COLS
+                cv = G_COLS + G_V_COLS
             else:
-                src = v_raw[g][:, :, c * CH : (c + 1) * CH]
-            wg = work.tile([P, CH, PACK], BF16, name="wg", tag="wg", bufs=4, align_bytes=64)
-            grouped_t[(j, g)] = wg
-            cv = V_COLS[kind]
+                wg = work.tile([P, CH, PACK], BF16, name="wg", tag="wg", bufs=4, align_bytes=64)
+                grouped_t[(j, g)] = wg
+                c0 = 0
+                cv = V_COLS[kind]
             nc.vector.tensor_copy(
-                out=wg[:, 0:cv, :].rearrange("p (c i) t -> p c t i", i=RUN),
-                in_=src[:, :, 0:cv].rearrange("p t (c i) -> p c t i", i=RUN),
+                out=wg[:, c0:cv, :].rearrange("p (c i) t -> p c t i", i=RUN),
+                in_=src[:, :, c0:cv].rearrange("p t (c i) -> p c t i", i=RUN),
             )
             if cv < CH:
                 nc.scalar.copy(
@@ -250,10 +283,11 @@ def tile_groupedqueryattention_pa_kernel(
                         out=junk[:], in_=acc[m][:, h * HD : (h + 1) * HD], func=ACT.Square,
                         accum_out=ssq[:, i : i + 1],
                     )
-            rms = work.tile([P, n], F32, name="rms", tag="rms", bufs=2)
-            nc.scalar.activation(out=rms[:], in_=ssq[:], func=ACT.Sqrt, scale=1.0 / HD, bias=EPS)
-            rstd = work.tile([P, n], F32, name="rstd", tag="rstd", bufs=2)
+            rms = rms_tiles[j % 2]
+            nc.scalar.activation(out=rms[:, 0:n], in_=ssq[:], func=ACT.Sqrt, scale=1.0 / HD, bias=EPS)
+            rstd = work.tile([P, n + 1], F32, name="rstd", tag="rstd", bufs=2)
             nc.vector.reciprocal(out=rstd[:], in_=rms[:])
+            early_interleave(j, rstd[:, n : n + 1])
             for m in range(M_TILES):
                 o = work.tile([P, HEADS_CH, HD], F32, name="o", tag="o", bufs=7)
                 for h in range(HEADS_CH):

@@ -31,8 +31,7 @@ FLOPS = 2 * T * D * (NQ + 2 * NKV)
 V_COLS = {"q": 512, "k": 256, "v": 256}
 RUN = 4
 V_WIDEN = ((1, 3), (3, 3))
-G_COLS = 320
-G_V_COLS = 64
+G_COLS = 384
 X_STEP = 5
 
 
@@ -206,17 +205,15 @@ def tile_groupedqueryattention_pa_kernel(
             src = planes(j, g)
             if (j, g) in grouped_t:
                 wg = grouped_t[(j, g)]
-                c0 = G_COLS
-                cv = G_COLS + G_V_COLS
+                cv = G_COLS
             else:
                 wg = work.tile([P, CH, PACK], BF16, name="wg", tag="wg", bufs=4, align_bytes=64)
                 grouped_t[(j, g)] = wg
-                c0 = 0
                 cv = V_COLS[kind]
-            nc.vector.tensor_copy(
-                out=wg[:, c0:cv, :].rearrange("p (c i) t -> p c t i", i=RUN),
-                in_=src[:, :, c0:cv].rearrange("p t (c i) -> p c t i", i=RUN),
-            )
+                nc.vector.tensor_copy(
+                    out=wg[:, 0:cv, :].rearrange("p (c i) t -> p c t i", i=RUN),
+                    in_=src[:, :, 0:cv].rearrange("p t (c i) -> p c t i", i=RUN),
+                )
             if cv < CH:
                 nc.scalar.copy(
                     out=wg[:, cv:CH, :].rearrange("p (c i) t -> p c t i", i=RUN),

@@ -28,9 +28,10 @@ EPS = 1e-6
 
 FLOPS = 2 * T * D * (NQ + 2 * NKV)
 
-V_COLS = {"q": 512, "k": 256, "v": 256}
+V_COLS = {"q": 512, "k": 272, "v": 272}
 RUN = 4
 V_WIDEN = ((1, 3), (3, 3))
+V_WIDEN_LATER = (0, 3)
 G_COLS = 384
 X_STEP = 5
 
@@ -166,7 +167,9 @@ def tile_groupedqueryattention_pa_kernel(
             wide_t[(j, g)] = wide
             for t in range(PACK):
                 src = q_bytes[g][:, t, c * CH : (c + 1) * CH].bitcast(FP8)
-                on_vector = (g, t) in V_WIDEN or (j == 0 and g == 0 and t >= 2)
+                on_vector = (
+                    (g, t) in V_WIDEN or (j == 0 and g == 0 and t >= 2) or (j >= 1 and (g, t) == V_WIDEN_LATER)
+                )
                 if on_vector:
                     nc.vector.tensor_scalar(
                         out=wide[:, t, :], in0=src, scalar1=q_scale_column(g, t), scalar2=None,

from contextlib import ExitStack

import concourse.mybir as mybir
from concourse.masks import make_identity

F32 = mybir.dt.float32
BF16 = mybir.dt.bfloat16
U32 = mybir.dt.uint32
U8 = mybir.dt.uint8
FP8 = mybir.dt.float8_e4m3fn
FP8X4 = mybir.dt.float8_e4m3fn_x4
ACT = mybir.ActivationFunctionType
ALU = mybir.AluOpType

P = 128
PACK = 4
K_PASS = P * PACK
T = 512
D = 2560
PASSES = D // K_PASS
M_TILES = T // P
HD = 256
CH = 512
HEADS_CH = CH // HD
NQ = 2048
NKV = 1024
EPS = 1e-6

FLOPS = 2 * T * D * (NQ + 2 * NKV)

V_COLS = {"q": 512, "k": 272, "v": 272}
RUN = 4
V_WIDEN = ((1, 3), (3, 3))
V_WIDEN_LATER = (0, 3)
G_COLS = 384
X_STEP = 5


def tile_groupedqueryattention_pa_kernel(
    tc, x, Wq_bytes, Wq_scale, Wk, Wv, q_scale, k_scale, out_0, out_1, out_2
):
    nc = tc.nc
    with ExitStack() as ctx:
        const = ctx.enter_context(tc.tile_pool(name="const", bufs=1))
        raw = ctx.enter_context(tc.tile_pool(name="raw", bufs=1))
        work = ctx.enter_context(tc.tile_pool(name="work", bufs=2))
        psum = ctx.enter_context(tc.psum_pool(name="psum", bufs=2))
        ctx.enter_context(tc.manual_schedule(engines={mybir.EngineType.SP}))

        qs_view = Wq_scale.rearrange("(g p t) o -> p g (t o)", p=P, t=PACK)
        qs_first = const.tile([P, 1, PACK], F32, name="qs_first")
        nc.scalar.dma_start(out=qs_first[:], in_=qs_view[:, 0:1, :])
        qs_rest = const.tile([P, PASSES - 1, PACK], F32, name="qs_rest")
        nc.scalar.dma_start(out=qs_rest[:], in_=qs_view[:, 1:PASSES, :])

        def q_scale_column(g, t):
            if g == 0:
                return qs_first[:, 0, t : t + 1]
            return qs_rest[:, g - 1, t : t + 1]

        warm = const.tile([P, 1], F32, name="warm")
        nc.vector.memset(warm[:], 1.0)
        nc.scalar.activation(out=warm[:], in_=warm[:], func=ACT.Sqrt)

        gain_rows = const.tile([P, 2 * HD], BF16, name="gain_rows")
        nc.gpsimd.memset(gain_rows[:], 0.0)
        nc.scalar.dma_start(out=gain_rows[0:1, 0:HD], in_=q_scale.rearrange("(o d) -> o d", o=1))
        nc.scalar.dma_start(out=gain_rows[0:1, HD : 2 * HD], in_=k_scale.rearrange("(o d) -> o d", o=1))

        wq_view = Wq_bytes.rearrange("(g p t) n -> g p t n", p=P, t=PACK)
        wk_view = Wk.rearrange("(g p t) n -> g p t n", p=P, t=PACK)
        wv_view = Wv.rearrange("(g p t) n -> g p t n", p=P, t=PACK)
        x_view = x.rearrange("b (m p) k -> p (b m) k", p=P)

        q_bytes = [raw.tile([P, PACK, NQ], U8, name="q_bytes%d" % g, tag="qv%d" % g) for g in range(PASSES)]
        x_raw = [raw.tile([P, M_TILES, K_PASS], BF16, name="x_raw%d" % g) for g in range(PASSES)]
        k_raw = [raw.tile([P, PACK, NKV], BF16, name="k_raw%d" % g) for g in range(PASSES)]
        v_raw = []

        half = NQ // 2
        for t0 in (0, 2):
            nc.sync.dma_start(out=q_bytes[0][:, t0 : t0 + 2, 0:half], in_=wq_view[0][:, t0 : t0 + 2, 0:half])
        for g in range(1, PASSES):
            nc.sync.dma_start(out=q_bytes[g][:, :, 0:half], in_=wq_view[g][:, :, 0:half])
        for g in range(PASSES):
            nc.sync.dma_start(out=x_raw[g][:], in_=x_view[:, :, g * K_PASS : (g + 1) * K_PASS])
        nc.sync.dma_start(out=k_raw[0][:], in_=wk_view[0])
        for g in range(PASSES):
            nc.sync.dma_start(out=q_bytes[g][:, :, half:NQ], in_=wq_view[g][:, :, half:NQ])

        def late_loads(j):
            if j == 0:
                for g in range(1, PASSES):
                    nc.sync.dma_start(out=k_raw[g][:], in_=wk_view[g])
            if j == 2:
                for g in range(PASSES):
                    v_raw.append(raw.tile([P, PACK, NKV], BF16, name="v_raw%d" % g, tag="qv%d" % g))
                    nc.sync.dma_start(out=v_raw[g][:], in_=wv_view[g])

        ident = const.tile([P, P], F32, name="ident")
        make_identity(nc, ident[:])
        ones = const.tile([P, P], BF16, name="ones")
        nc.gpsimd.memset(ones[:], 1.0)
        gain_all = const.tile([P, 2 * HD], F32, name="gain_all")
        gain = {"q": gain_all[:, 0:HD], "k": gain_all[:, HD : 2 * HD]}

        def spread_gains():
            gain_ps = psum.tile([P, 2 * HD], F32, name="gain_ps", tag="bank", bufs=8)
            nc.tensor.matmul(out=gain_ps[:], lhsT=ones[:], rhs=gain_rows[:], start=True, stop=True)
            nc.vector.tensor_scalar(
                out=gain_all[:], in0=gain_ps[:], scalar1=1.0, scalar2=None, op0=ALU.add
            )

        n_sums = M_TILES * HEADS_CH
        rms_tiles = [const.tile([P, n_sums + 1], F32, name="rms%d" % i) for i in range(2)]
        for i in range(2):
            nc.gpsimd.memset(rms_tiles[i][:], 1.0)

        x_codes = const.tile([P, PASSES, T], U32, name="x_codes", align_bytes=64)
        x_scales = const.tile([P, PASSES, T], U8, name="x_scales", align_bytes=64)

        x_grouped = {}

        def x_turn(g):
            xg = work.tile([P, T, PACK], BF16, name="xg", tag="xg", bufs=2, align_bytes=64)
            x_grouped[g] = xg
            xg_words = (
                xg[:].rearrange("p r j -> p (r j)").bitcast(F32)
                .rearrange("p (m r u) -> p m r u", m=M_TILES, u=2)
            )
            for pair in range(M_TILES // 2):
                xt = psum.tile([P, 2, 2, P], F32, name="xt", tag="bank", bufs=8)
                for mm in range(2):
                    words = x_raw[g][:, 2 * pair + mm, :].bitcast(F32)
                    for u in range(2):
                        nc.tensor.transpose(xt[:, mm, u, :], words[:, u : K_PASS // 2 : 2], ident[:])
                dst = xg_words[:, 2 * pair : 2 * pair + 2]
                src = xt[:].rearrange("p m u r -> p m r u")
                if pair == 0:
                    nc.scalar.copy(out=dst, in_=src)
                else:
                    nc.vector.tensor_copy(out=dst, in_=src)

        def x_quant(g):
            nc.vector.quantize_mx(
                out=x_codes[:, g, :].bitcast(FP8X4),
                scales=x_scales[:, g, :],
                in_=x_grouped[g][:].rearrange("p r j -> p (r j)"),
            )

        chunks = (
            [("q", c) for c in range(NQ // CH)]
            + [("k", c) for c in range(NKV // CH)]
            + [("v", c) for c in range(NKV // CH)]
        )
        units = [(j, g) for j in range(len(chunks)) for g in range(PASSES)]
        wide_t = {}
        grouped_t = {}
        codes_t = {}
        acc_t = {}

        def widen(j, g):
            kind, c = chunks[j]
            if kind != "q":
                return
            wide = work.tile([P, PACK, CH], BF16, name="wide", tag="wide", bufs=6)
            wide_t[(j, g)] = wide
            for t in range(PACK):
                src = q_bytes[g][:, t, c * CH : (c + 1) * CH].bitcast(FP8)
                on_vector = (
                    (g, t) in V_WIDEN or (j == 0 and g == 0 and t >= 2) or (j >= 1 and (g, t) == V_WIDEN_LATER)
                )
                if on_vector:
                    nc.vector.tensor_scalar(
                        out=wide[:, t, :], in0=src, scalar1=q_scale_column(g, t), scalar2=None,
                        op0=ALU.mult,
                    )
                else:
                    nc.scalar.activation(
                        out=wide[:, t, :], in_=src, func=ACT.Copy, scale=q_scale_column(g, t)
                    )

        def planes(j, g):
            kind, c = chunks[j]
            if kind == "q":
                return wide_t[(j, g)][:]
            if kind == "k":
                return k_raw[g][:, :, c * CH : (c + 1) * CH]
            return v_raw[g][:, :, c * CH : (c + 1) * CH]

        def early_unit(j):
            first_plain = NQ // CH
            if j + 2 <= first_plain:
                return (first_plain, j)
            return (j + 2, 0)

        def early_interleave(j, one):
            u = early_unit(j)
            wg = work.tile([P, CH, PACK], BF16, name="wg_early", tag="wg_early", bufs=4, align_bytes=64)
            grouped_t[u] = wg
            nc.gpsimd.tensor_scalar(
                out=wg[:, 0:G_COLS, :], in0=planes(*u)[:, :, 0:G_COLS].rearrange("p t c -> p c t"),
                scalar1=one, scalar2=0.0, op0=ALU.mult, op1=ALU.add,
            )

        def interleave(j, g):
            kind, c = chunks[j]
            src = planes(j, g)
            if (j, g) in grouped_t:
                wg = grouped_t[(j, g)]
                cv = G_COLS
            else:
                wg = work.tile([P, CH, PACK], BF16, name="wg", tag="wg", bufs=4, align_bytes=64)
                grouped_t[(j, g)] = wg
                cv = V_COLS[kind]
                nc.vector.tensor_copy(
                    out=wg[:, 0:cv, :].rearrange("p (c i) t -> p c t i", i=RUN),
                    in_=src[:, :, 0:cv].rearrange("p t (c i) -> p c t i", i=RUN),
                )
            if cv < CH:
                nc.scalar.copy(
                    out=wg[:, cv:CH, :].rearrange("p (c i) t -> p c t i", i=RUN),
                    in_=src[:, :, cv:CH].rearrange("p t (c i) -> p c t i", i=RUN),
                )

        def quantize(j, g):
            if g == 0:
                wc = work.tile([P, PASSES, CH], U32, name="wc", tag="wc", bufs=2, align_bytes=64)
                ws = work.tile([P, PASSES, CH], U8, name="ws", tag="ws", bufs=2, align_bytes=64)
                codes_t[j] = (wc, ws)
            wc, ws = codes_t[j]
            nc.vector.quantize_mx(
                out=wc[:, g, :].bitcast(FP8X4),
                scales=ws[:, g, :],
                in_=grouped_t[(j, g)][:].rearrange("p c t -> p (c t)"),
            )

        def matmuls(j, g):
            if g == 0:
                acc_t[j] = [
                    psum.tile([P, CH], F32, name="acc", tag="bank", bufs=8) for m in range(M_TILES)
                ]
            wc, ws = codes_t[j]
            for m in range(M_TILES):
                cols = slice(m * P, (m + 1) * P)
                nc.tensor.matmul_mx(
                    out=acc_t[j][m][:],
                    lhsT=x_codes[:, g, cols].bitcast(FP8X4),
                    lhsT_scale=x_scales[:, g, cols],
                    rhs=wc[:, g, :].bitcast(FP8X4),
                    rhs_scale=ws[:, g, :],
                    start=(g == 0),
                    stop=(g == PASSES - 1),
                )

        out_views = {
            "q": out_0.rearrange("b h (m p) d -> p (b h) m d", p=P),
            "k": out_1.rearrange("b h (m p) d -> p (b h) m d", p=P),
            "v": out_2.rearrange("b h (m p) d -> p (b h) m d", p=P),
        }

        def epilogue(j):
            kind, c = chunks[j]
            acc = acc_t[j]
            heads = slice(c * HEADS_CH, (c + 1) * HEADS_CH)
            if kind == "v":
                for m in range(M_TILES):
                    o = work.tile([P, HEADS_CH, HD], F32, name="o", tag="o", bufs=7)
                    flat = o[:].rearrange("p h d -> p (h d)")
                    if m % 2 == 0 or j < len(chunks) - 1:
                        nc.scalar.copy(out=flat, in_=acc[m][:])
                    else:
                        nc.vector.tensor_copy(out=flat, in_=acc[m][:])
                    nc.sync.dma_start(out=out_views[kind][:, heads, m, :], in_=o[:])
                return
            n = M_TILES * HEADS_CH
            ssq = work.tile([P, n], F32, name="ssq", tag="ssq", bufs=2)
            for m in range(M_TILES):
                for h in range(HEADS_CH):
                    junk = work.tile([P, HD], BF16, name="junk", tag="junk", bufs=2)
                    i = m * HEADS_CH + h
                    nc.scalar.activation(
                        out=junk[:], in_=acc[m][:, h * HD : (h + 1) * HD], func=ACT.Square,
                        accum_out=ssq[:, i : i + 1],
                    )
            rms = rms_tiles[j % 2]
            nc.scalar.activation(out=rms[:, 0:n], in_=ssq[:], func=ACT.Sqrt, scale=1.0 / HD, bias=EPS)
            rstd = work.tile([P, n + 1], F32, name="rstd", tag="rstd", bufs=2)
            nc.vector.reciprocal(out=rstd[:], in_=rms[:])
            early_interleave(j, rstd[:, n : n + 1])
            for m in range(M_TILES):
                o = work.tile([P, HEADS_CH, HD], F32, name="o", tag="o", bufs=7)
                for h in range(HEADS_CH):
                    i = m * HEADS_CH + h
                    nc.vector.scalar_tensor_tensor(
                        out=o[:, h, :], in0=acc[m][:, h * HD : (h + 1) * HD],
                        scalar=rstd[:, i : i + 1], in1=gain[kind],
                        op0=ALU.mult, op1=ALU.mult,
                    )
                nc.sync.dma_start(out=out_views[kind][:, heads, m, :], in_=o[:])

        n_units = len(units)
        waiting = []
        due = {}
        x_done = False
        for s in range(n_units + 5):
            if s < n_units:
                widen(*units[s])
            if 1 <= s <= n_units:
                interleave(*units[s - 1])
            if 2 <= s <= n_units + 1:
                quantize(*units[s - 2])
                waiting.append(units[s - 2])
            if s == X_STEP:
                for g in range(PASSES):
                    x_turn(g)
                    if g >= 1:
                        x_quant(g - 1)
                x_quant(PASSES - 1)
                spread_gains()
                x_done = True
            if x_done:
                for u in waiting:
                    matmuls(*u)
                    if u[1] == PASSES - 1:
                        due.setdefault(s + 1, []).append(u[0])
                waiting = []
            for j in due.get(s, []):
                epilogue(j)
                late_loads(j)
